import numpy as np
import ml_dtypes


def mxq(x, axis, fmt="e4m3"):
    dtype, down = {"e4m3": (ml_dtypes.float8_e4m3fn, 7), "e5m2": (ml_dtypes.float8_e5m2, 14)}[fmt]
    v = np.moveaxis(np.asarray(x, np.float32).astype(ml_dtypes.bfloat16).astype(np.float64), axis, -1)
    blocks = v.reshape(v.shape[:-1] + (-1, 32))
    amax = np.abs(blocks).max(-1, keepdims=True)
    byte = np.maximum(np.where(amax > 0, np.frexp(amax)[1] - 1 + 127, 0) - down, 1)
    scale = np.exp2(byte - 127.0)
    codes = (blocks / scale).astype(np.float32).astype(dtype).astype(np.float64)
    return np.moveaxis((codes * scale).reshape(v.shape), -1, axis)


WIDE = False


def mx_kscale(k):
    if not WIDE:
        return np.ones(k)
    levels = np.array([10, -10, 5, -5, 0])
    if k % 512:
        return np.exp2(np.random.permutation(np.resize(levels, k // 32))).repeat(32)
    a = np.empty((k // 512, 16))
    for p in range(k // 512):
        a[p, :8] = np.random.permutation(np.resize(levels, 8))
        for g in range(8):
            far = levels[np.abs(levels - a[p, g]) >= 10]
            a[p, g + 8] = far[np.random.randint(len(far))]
    return np.exp2(a.ravel()).repeat(32)


BF16 = ml_dtypes.bfloat16


def bf(x):
    return np.asarray(x, np.float32).astype(BF16)


def f64(x):
    return np.asarray(x).astype(np.float64)


B, N, C, H, REG, QKV, LAYERS, PAIR = 1, 1024, 1024, 8, 5, 3, 12, 2
D = C // H


def setup_inputs():
    s = mx_kscale(C)
    w = np.random.standard_normal((C, QKV * C)) * 1.5 / np.sqrt(C)
    m = np.random.standard_normal(C)
    al = np.random.standard_normal((B, N, 1))
    x = np.random.standard_normal((B, N, C)) + al * m
    gain = np.exp2(np.random.uniform(-1.0, 1.0, (H, 1)))
    g = ((m[:, None] * w[:, :C]).sum(0).reshape(H, D) + np.random.standard_normal((H, D))) * gain
    return {"x": bf(x * s), "W_qkv": bf(w / s[:, None]), "q_g": bf(g)}


def reference(x, W_qkv, q_g):
    qkv = (mxq(f64(x), 2, "e4m3") @ mxq(f64(W_qkv), 0, "e4m3")).reshape(B, N, QKV, H, D)
    q, k, v = qkv[:, :, 0], qkv[:, :, 1], qkv[:, :, 2]
    q_pure = q[:, REG:]
    q_n = q_pure / np.sqrt((q_pure ** 2).sum(-1, keepdims=True))
    g = f64(q_g)
    qg_n = g / np.sqrt((g ** 2).sum(-1, keepdims=True))
    sim = (qg_n[None, None] * q_n).sum(-1).mean(-1)
    return q, k, v, sim

@@ -1,0 +1,476 @@
+from contextlib import ExitStack
+
+import concourse.mybir as mybir
+from concourse.masks import make_identity
+
+F32 = mybir.dt.float32
+BF16 = mybir.dt.bfloat16
+U32 = mybir.dt.uint32
+U8 = mybir.dt.uint8
+FP8X4 = mybir.dt.float8_e4m3fn_x4
+ACT = mybir.ActivationFunctionType
+ALU = mybir.AluOpType
+AX = mybir.AxisListType
+
+P = 128
+N_TOK = 1024
+C = 1024
+H = 8
+D = 128
+REG = 5
+T = N_TOK // P
+HALF = 512
+FINE = 6
+FLOPS = 2 * N_TOK * C * 3 * C
+
+
+def tile_memeffattention_pa_kernel(tc, x, W_qkv, q_g, out_0, out_1, out_2, out_3):
+    nc = tc.nc
+    with ExitStack() as ctx:
+        const = ctx.enter_context(tc.tile_pool(name="const", bufs=1))
+        wraw_pool = ctx.enter_context(tc.tile_pool(name="wraw", bufs=3))
+        wg_pool = ctx.enter_context(tc.tile_pool(name="wg", bufs=4))
+        xg_pool = ctx.enter_context(tc.tile_pool(name="xg", bufs=2))
+        kv_pool = ctx.enter_context(tc.tile_pool(name="kv", bufs=8))
+        psum = ctx.enter_context(tc.psum_pool(name="psum", bufs=8))
+        ctx.enter_context(tc.manual_schedule())
+
+        xv = x.flatten_outer_dims().rearrange("(p t) k -> p t k", t=T)
+        outs = [
+            o.rearrange("b n h d -> (b n) (h d)").rearrange("(p t) f -> p t f", t=T)
+            for o in (out_0, out_1, out_2)
+        ]
+
+        def on(eng):
+            return nc.vector.tensor_copy if eng == "v" else nc.scalar.copy
+
+        grow = const.tile([P, C], BF16, name="grow")
+        nc.vector.memset(grow[:], 0.0)
+        x_sb = const.tile([P, T * C], BF16, name="x_sb")
+        x_sb3 = x_sb[:].rearrange("p (t k) -> p t k", t=T)
+        xw = x_sb[:].bitcast(F32).rearrange("p (t w) -> p t w", t=T)
+        wraw = [
+            wraw_pool.tile([P, 2, 2, 2, C], BF16, name="wraw%d" % s, tag="wraw") for s in range(3)
+        ]
+        ident = const.tile([P, P], F32, name="ident")
+        make_identity(nc, ident[:])
+        ones = const.tile([P, P], BF16, name="ones")
+        nc.vector.memset(ones[:], 1.0)
+        warm = const.tile([P, 2], F32, name="warm")
+        nc.vector.memset(warm[:], 1.0)
+        nc.scalar.activation(out=warm[:, 1:2], in_=warm[:, 0:1], func=ACT.Sqrt)
+        blk_m = const.tile([P, P], F32, name="blk_m")
+        nc.vector.memset(blk_m[:], 0.0)
+        lane = const.tile([P, 16, 1], F32, name="lane")
+        xc = const.tile([P, T * 2 * P], U32, name="xc", align_bytes=64)
+        xs = const.tile([P, T * 2 * P], U8, name="xs", align_bytes=64)
+        wc = const.tile([P, 3 * 2 * C], U32, name="wc", align_bytes=64)
+        ws = const.tile([P, 3 * 2 * C], U8, name="ws", align_bytes=64)
+        q_sb = const.tile([P, T, C], F32, name="q_sb")
+        g_sb = const.tile([P, C], F32, name="g_sb")
+        qq = const.tile([P, T * H], F32, name="qq")
+        qd = const.tile([P, T * H], F32, name="qd")
+        gg_t = const.tile([P, H], F32, name="gg_t")
+        junk_s = const.tile([P, H, D], F32, name="junk_s")
+        junk_v = const.tile([P, H, D], F32, name="junk_v")
+        gn_t = const.tile([P, 1, H], F32, name="gn_t")
+        qn_t = const.tile([P, T, H], F32, name="qn_t")
+        den = const.tile([P, T, H], F32, name="den")
+        sim = const.tile([P, 1, T], F32, name="sim")
+        spread = const.tile([P, 16, T], F32, name="spread")
+        rows_t = const.tile([P, P], F32, name="rows_t")
+        live = {}
+        done = {"sq": 0, "dot": 0, "gg": 0}
+
+        def ldw(s, c, u):
+            rows_c = W_qkv[512 * c : 512 * c + 512, s * C : (s + 1) * C].rearrange("(q j) n -> q j n", j=4)
+            nc.sync.dma_start(out=wraw[s][:, c, u, :, :], in_=rows_c[:, 2 * u : 2 * u + 2, :])
+
+        def ldx(t0, nt):
+            nc.sync.dma_start(out=x_sb3[:, t0 : t0 + nt, :], in_=xv[:, t0 : t0 + nt, :])
+
+        def ldg():
+            nc.sync.dma_start(out=grow[0:1, :], in_=q_g.rearrange("(o h) d -> o (h d)", o=1))
+
+        def masks():
+            nc.vector.tensor_reduce(
+                out=blk_m[:, 0:8], in_=ident[:].rearrange("p (m b) -> p m b", b=16), axis=AX.X, op=ALU.add
+            )
+            nc.vector.tensor_reduce(
+                out=lane[:, :, 0], in_=ident[:].rearrange("p (m b) -> p b m", b=16), axis=AX.X, op=ALU.add
+            )
+
+        def gmm(h):
+            gp = psum.tile([P, HALF], F32, name="gp", tag="bank")
+            nc.tensor.matmul(
+                out=gp[:], lhsT=ones[:], rhs=grow[:, h * HALF : (h + 1) * HALF], start=True, stop=True
+            )
+            live[("gp", h)] = gp
+
+        def gex(h, eng):
+            on(eng)(out=g_sb[:, h * HALF : (h + 1) * HALF], in_=live[("gp", h)][:])
+
+        def rg(s, c, h, eng):
+            g = wg_pool.tile([P, 4 * HALF], BF16, name="wg", tag="wg", align_bytes=64)
+            src = wraw[s][:, c].rearrange("p u e n -> p (u e) n")[:, :, h * HALF : (h + 1) * HALF]
+            on(eng)(
+                out=g[:].rearrange("p (a i j) -> p a j i", i=4, j=4),
+                in_=src.rearrange("p j (a i) -> p a j i", i=4),
+            )
+            live[("wg", s, c, h)] = g
+
+        def qz(s, c, h):
+            o = (s * 2 + c) * C + h * HALF
+            nc.vector.quantize_mx(
+                out=wc[:, o : o + HALF].bitcast(FP8X4),
+                scales=ws[:, o : o + HALF],
+                in_=live[("wg", s, c, h)][:],
+            )
+
+        def xT(t):
+            xt = psum.tile([P, 2, 2, P], F32, name="xt", tag="bank")
+            for c in range(2):
+                for u in range(2):
+                    nc.tensor.transpose(
+                        xt[:, c, u, :], xw[:, t, 256 * c + u : 256 * (c + 1) : 2], ident[:]
+                    )
+            live[("xt", t)] = xt
+
+        def xe(t, eng):
+            if t % 2 == 0:
+                live[("xg", t // 2)] = xg_pool.tile(
+                    [P, 2 * 2 * P * 4], BF16, name="xg", tag="xg", align_bytes=64
+                )
+            xgw = live[("xg", t // 2)][:].bitcast(F32).rearrange(
+                "p (t c m u) -> p t c m u", t=2, c=2, u=2
+            )
+            on(eng)(out=xgw[:, t % 2], in_=live[("xt", t)][:].rearrange("p c u m -> p c m u"))
+
+        def xq(t0, nt):
+            a = (t0 % 2) * 1024
+            nc.vector.quantize_mx(
+                out=xc[:, t0 * 256 : (t0 + nt) * 256].bitcast(FP8X4),
+                scales=xs[:, t0 * 256 : (t0 + nt) * 256],
+                in_=live[("xg", t0 // 2)][:, a : a + nt * 1024],
+            )
+
+        def mx(b):
+            s, t, h = b // 16, (b % 16) // 2, b % 2
+            acc = psum.tile([P, HALF], F32, name="acc", tag="bank")
+            for c in range(2):
+                xo = (t * 2 + c) * P
+                wo = (s * 2 + c) * C + h * HALF
+                nc.tensor.matmul_mx(
+                    out=acc[:],
+                    lhsT=xc[:, xo : xo + P].bitcast(FP8X4),
+                    lhsT_scale=xs[:, xo : xo + P],
+                    rhs=wc[:, wo : wo + HALF].bitcast(FP8X4),
+                    rhs_scale=ws[:, wo : wo + HALF],
+                    start=(c == 0),
+                    stop=(c == 1),
+                )
+            live[("acc", b)] = acc
+
+        def ex(b, eng):
+            s, t, h = b // 16, (b % 16) // 2, b % 2
+            cols = slice(h * HALF, (h + 1) * HALF)
+            if s == 0:
+                row = q_sb[:, t, :]
+            else:
+                if h == 0:
+                    live[("st", s, t)] = kv_pool.tile([P, C], F32, name="stage", tag="stage")
+                row = live[("st", s, t)][:]
+            on(eng)(out=row[:, cols], in_=live[("acc", b)][:])
+            if s == 2 and t >= FINE:
+                nc.sync.dma_start(out=outs[s][:, t, cols], in_=row[:, cols])
+            elif h == 1:
+                nc.sync.dma_start(out=outs[s][:, t, :], in_=row)
+
+        def dot_v(a, b, acc1, slot):
+            nc.vector.scalar_tensor_tensor(
+                out=junk_v[:, slot, :], in0=a, scalar=1.0, in1=b,
+                op0=ALU.mult, op1=ALU.mult, accum_out=acc1,
+            )
+
+        def gg(n):
+            for r in range(n):
+                hd = done["gg"]
+                done["gg"] = hd + 1
+                gh = g_sb[:, hd * D : (hd + 1) * D]
+                dot_v(gh, gh, gg_t[:, hd : hd + 1], hd)
+
+        def dot(n):
+            for r in range(n):
+                k = done["dot"]
+                done["dot"] = k + 1
+                t, hd = k // H, k % H
+                dot_v(q_sb[:, t, hd * D : (hd + 1) * D], g_sb[:, hd * D : (hd + 1) * D], qd[:, k : k + 1], hd)
+
+        def sq(n):
+            for r in range(n):
+                k = done["sq"]
+                done["sq"] = k + 1
+                t, hd = k // H, k % H
+                nc.scalar.activation(
+                    out=junk_s[:, hd, :], in_=q_sb[:, t, hd * D : (hd + 1) * D], func=ACT.Square,
+                    accum_out=qq[:, k : k + 1],
+                )
+
+        def gn():
+            nc.scalar.activation(out=gn_t[:, 0, :], in_=gg_t[:], func=ACT.Sqrt, scale=float(H * H))
+
+        def qn():
+            nc.scalar.activation(out=qn_t[:].rearrange("p t h -> p (t h)"), in_=qq[:], func=ACT.Sqrt)
+
+        def chain():
+            nc.vector.tensor_tensor(out=den[:], in0=qn_t[:], in1=gn_t[:].to_broadcast([P, T, H]), op=ALU.mult)
+            nc.vector.reciprocal(out=den[:], in_=den[:])
+            nc.vector.tensor_tensor(
+                out=den[:], in0=den[:], in1=qd[:].rearrange("p (t h) -> p t h", h=H), op=ALU.mult
+            )
+            nc.vector.tensor_reduce(out=sim[:, 0, :], in_=den[:], axis=AX.X, op=ALU.add)
+            nc.vector.tensor_tensor(
+                out=spread[:], in0=sim[:].to_broadcast([P, 16, T]), in1=lane[:].to_broadcast([P, 16, T]),
+                op=ALU.mult,
+            )
+
+        def blk():
+            sp = psum.tile([P, P], F32, name="sp", tag="bank")
+            nc.tensor.matmul(
+                out=sp[:], lhsT=blk_m[:], rhs=spread[:].rearrange("p b t -> p (b t)"), start=True, stop=True
+            )
+            live["sp"] = sp
+
+        def rows(eng):
+            on(eng)(out=rows_t[:], in_=live["sp"][:])
+
+        def stsim():
+            nc.sync.dma_start(out=out_3[0:1, 0 : P - REG], in_=rows_t[0:1, REG:P])
+            nc.sync.dma_start(
+                out=out_3[0:1, P - REG : N_TOK - REG].rearrange("o (m j) -> (o m) j", j=P),
+                in_=rows_t[1:8, :],
+            )
+
+        ldw(0, 0, 0)
+        ldw(0, 0, 1)
+        ldw(0, 1, 0)
+        ldw(0, 1, 1)
+        ldx(0, 1)
+        ldx(1, 1)
+        ldx(2, 2)
+        ldx(4, 2)
+        ldx(6, 2)
+        ldw(1, 0, 0)
+        ldw(1, 0, 1)
+        ldw(1, 1, 0)
+        ldw(1, 1, 1)
+        ldg()
+        ldw(2, 0, 0)
+        ldw(2, 0, 1)
+        ldw(2, 1, 0)
+        ldw(2, 1, 1)
+        rg(0, 0, 0, "v")
+        rg(0, 0, 1, "s")
+        masks()
+        qz(0, 0, 0)
+        rg(0, 1, 0, "v")
+        rg(0, 1, 1, "s")
+        qz(0, 0, 1)
+        qz(0, 1, 0)
+        xT(0)
+        xT(1)
+        xT(2)
+        xT(3)
+        xT(4)
+        xT(5)
+        xe(0, "v")
+        xe(1, "s")
+        qz(0, 1, 1)
+        xq(0, 2)
+        mx(0)
+        mx(1)
+        xe(2, "s")
+        xe(3, "s")
+        mx(2)
+        mx(3)
+        xq(2, 2)
+        xT(6)
+        xT(7)
+        xe(4, "s")
+        xe(5, "s")
+        xq(4, 2)
+        mx(4)
+        mx(5)
+        ex(0, "s")
+        mx(6)
+        ex(1, "s")
+        mx(7)
+        xe(6, "s")
+        xe(7, "v")
+        rg(1, 0, 0, "v")
+        ex(2, "s")
+        mx(8)
+        xq(6, 2)
+        ex(3, "s")
+        mx(9)
+        ex(4, "s")
+        mx(10)
+        rg(1, 0, 1, "v")
+        ex(5, "s")
+        mx(11)
+        qz(1, 0, 0)
+        ex(6, "s")
+        mx(12)
+        rg(1, 1, 0, "v")
+        gmm(0)
+        gmm(1)
+        ex(7, "s")
+        mx(13)
+        qz(1, 0, 1)
+        ex(8, "s")
+        mx(14)
+        sq(2)
+        rg(1, 1, 1, "v")
+        gex(0, "s")
+        gex(1, "s")
+        ex(9, "s")
+        mx(15)
+        sq(2)
+        qz(1, 1, 0)
+        qz(1, 1, 1)
+        ex(10, "s")
+        mx(16)
+        sq(2)
+        ex(11, "s")
+        mx(17)
+        sq(2)
+        ex(12, "s")
+        mx(18)
+        sq(2)
+        ex(13, "s")
+        mx(19)
+        sq(2)
+        ex(14, "s")
+        mx(20)
+        sq(2)
+        ex(15, "s")
+        mx(21)
+        sq(2)
+        rg(2, 0, 0, "v")
+        gg(2)
+        rg(2, 1, 0, "v")
+        ex(16, "s")
+        mx(22)
+        sq(2)
+        qz(2, 0, 0)
+        gg(2)
+        ex(17, "s")
+        mx(23)
+        sq(2)
+        qz(2, 1, 0)
+        rg(2, 0, 1, "v")
+        ex(18, "s")
+        mx(24)
+        sq(2)
+        gg(2)
+        rg(2, 1, 1, "v")
+        ex(19, "s")
+        mx(25)
+        sq(2)
+        qz(2, 0, 1)
+        gg(2)
+        ex(20, "s")
+        mx(26)
+        sq(2)
+        qz(2, 1, 1)
+        ex(21, "s")
+        mx(27)
+        sq(2)
+        gn()
+        dot(3)
+        ex(22, "s")
+        mx(28)
+        sq(2)
+        dot(3)
+        ex(23, "v")
+        mx(29)
+        dot(3)
+        ex(24, "s")
+        mx(30)
+        sq(2)
+        dot(3)
+        ex(25, "s")
+        mx(31)
+        sq(2)
+        dot(3)
+        ex(26, "s")
+        mx(32)
+        sq(3)
+        dot(3)
+        ex(27, "v")
+        mx(33)
+        dot(3)
+        ex(28, "s")
+        mx(34)
+        sq(2)
+        dot(3)
+        ex(29, "s")
+        mx(35)
+        sq(3)
+        dot(3)
+        ex(30, "s")
+        mx(36)
+        sq(2)
+        dot(3)
+        ex(31, "v")
+        mx(37)
+        dot(3)
+        ex(32, "s")
+        mx(38)
+        sq(3)
+        dot(3)
+        ex(33, "s")
+        mx(39)
+        sq(2)
+        dot(3)
+        ex(34, "s")
+        mx(40)
+        sq(3)
+        dot(3)
+        ex(35, "v")
+        mx(41)
+        dot(3)
+        ex(36, "s")
+        mx(42)
+        sq(2)
+        dot(3)
+        ex(37, "s")
+        mx(43)
+        sq(3)
+        dot(3)
+        ex(38, "s")
+        mx(44)
+        sq(2)
+        dot(3)
+        ex(39, "v")
+        mx(45)
+        dot(3)
+        ex(40, "s")
+        mx(46)
+        sq(3)
+        dot(4)
+        ex(41, "s")
+        mx(47)
+        sq(2)
+        qn()
+        dot(3)
+        ex(42, "s")
+        ex(43, "v")
+        chain()
+        blk()
+        ex(44, "s")
+        rows("s")
+        stsim()
+        ex(45, "v")
+        ex(46, "s")
+        ex(47, "v")

@@ -28,10 +28,9 @@ def tile_memeffattention_pa_kernel(tc, x, W_qkv, q_g, out_0, out_1, out_2, out_3
     nc = tc.nc
     with ExitStack() as ctx:
         const = ctx.enter_context(tc.tile_pool(name="const", bufs=1))
-        wraw_pool = ctx.enter_context(tc.tile_pool(name="wraw", bufs=3))
         wg_pool = ctx.enter_context(tc.tile_pool(name="wg", bufs=4))
         xg_pool = ctx.enter_context(tc.tile_pool(name="xg", bufs=2))
-        kv_pool = ctx.enter_context(tc.tile_pool(name="kv", bufs=8))
+        kv_pool = ctx.enter_context(tc.tile_pool(name="kv", bufs=12))
         psum = ctx.enter_context(tc.psum_pool(name="psum", bufs=8))
         ctx.enter_context(tc.manual_schedule())
 
@@ -46,16 +45,20 @@ def tile_memeffattention_pa_kernel(tc, x, W_qkv, q_g, out_0, out_1, out_2, out_3
 
         grow = const.tile([P, C], BF16, name="grow")
         nc.vector.memset(grow[:], 0.0)
+        g8 = const.tile([P, D], BF16, name="g8")
+        nc.vector.memset(g8[:], 0.0)
         x_sb = const.tile([P, T * C], BF16, name="x_sb")
         x_sb3 = x_sb[:].rearrange("p (t k) -> p t k", t=T)
         xw = x_sb[:].bitcast(F32).rearrange("p (t w) -> p t w", t=T)
-        wraw = [
-            wraw_pool.tile([P, 2, 2, 2, C], BF16, name="wraw%d" % s, tag="wraw") for s in range(3)
-        ]
+        wq_raw = const.tile([P, 2, 2, 4, HALF], BF16, name="wq_raw")
+        wk_raw = const.tile([P, 2, 4, C], BF16, name="wk_raw")
+        wv_raw = const.tile([P, 2, 4, C], BF16, name="wv_raw")
         ident = const.tile([P, P], F32, name="ident")
         make_identity(nc, ident[:])
         ones = const.tile([P, P], BF16, name="ones")
         nc.vector.memset(ones[:], 1.0)
+        ones_f = const.tile([P, P], F32, name="ones_f")
+        nc.vector.memset(ones_f[:], 1.0)
         warm = const.tile([P, 2], F32, name="warm")
         nc.vector.memset(warm[:], 1.0)
         nc.scalar.activation(out=warm[:, 1:2], in_=warm[:, 0:1], func=ACT.Sqrt)
@@ -67,10 +70,11 @@ def tile_memeffattention_pa_kernel(tc, x, W_qkv, q_g, out_0, out_1, out_2, out_3
         wc = const.tile([P, 3 * 2 * C], U32, name="wc", align_bytes=64)
         ws = const.tile([P, 3 * 2 * C], U8, name="ws", align_bytes=64)
         q_sb = const.tile([P, T, C], F32, name="q_sb")
-        g_sb = const.tile([P, C], F32, name="g_sb")
+        g_sb = const.tile([P, C], BF16, name="g_sb")
         qq = const.tile([P, T * H], F32, name="qq")
         qd = const.tile([P, T * H], F32, name="qd")
-        gg_t = const.tile([P, H], F32, name="gg_t")
+        gg_c = const.tile([P, 1], F32, name="gg_c")
+        gg_d = const.tile([P, H], F32, name="gg_d")
         junk_s = const.tile([P, H, D], F32, name="junk_s")
         junk_v = const.tile([P, H, D], F32, name="junk_v")
         gn_t = const.tile([P, 1, H], F32, name="gn_t")
@@ -80,17 +84,24 @@ def tile_memeffattention_pa_kernel(tc, x, W_qkv, q_g, out_0, out_1, out_2, out_3
         spread = const.tile([P, 16, T], F32, name="spread")
         rows_t = const.tile([P, P], F32, name="rows_t")
         live = {}
-        done = {"sq": 0, "dot": 0, "gg": 0}
+        done = {"sq": 0, "dot": 0}
 
-        def ldw(s, c, u):
-            rows_c = W_qkv[512 * c : 512 * c + 512, s * C : (s + 1) * C].rearrange("(q j) n -> q j n", j=4)
-            nc.sync.dma_start(out=wraw[s][:, c, u, :, :], in_=rows_c[:, 2 * u : 2 * u + 2, :])
+        def w_rows(s, c):
+            return W_qkv[512 * c : 512 * c + 512, s * C : (s + 1) * C].rearrange("(q j) n -> q j n", j=4)
+
+        def ldwh(s, c, h):
+            nc.sync.dma_start(out=wq_raw[:, c, h, :, :], in_=w_rows(s, c)[:, :, h * HALF : (h + 1) * HALF])
+
+        def ldwc(s, c):
+            raw = wk_raw if s == 1 else wv_raw
+            nc.sync.dma_start(out=raw[:, c, :, :], in_=w_rows(s, c))
 
         def ldx(t0, nt):
             nc.sync.dma_start(out=x_sb3[:, t0 : t0 + nt, :], in_=xv[:, t0 : t0 + nt, :])
 
         def ldg():
             nc.sync.dma_start(out=grow[0:1, :], in_=q_g.rearrange("(o h) d -> o (h d)", o=1))
+            nc.sync.dma_start(out=g8[0:H, :], in_=q_g)
 
         def masks():
             nc.vector.tensor_reduce(
@@ -100,19 +111,29 @@ def tile_memeffattention_pa_kernel(tc, x, W_qkv, q_g, out_0, out_1, out_2, out_3
                 out=lane[:, :, 0], in_=ident[:].rearrange("p (m b) -> p b m", b=16), axis=AX.X, op=ALU.add
             )
 
-        def gmm(h):
-            gp = psum.tile([P, HALF], F32, name="gp", tag="bank")
-            nc.tensor.matmul(
-                out=gp[:], lhsT=ones[:], rhs=grow[:, h * HALF : (h + 1) * HALF], start=True, stop=True
-            )
-            live[("gp", h)] = gp
+        def gmm1():
+            gp = psum.tile([P, C], BF16, name="gp", tag="bank")
+            for h in range(2):
+                cols = slice(h * HALF, (h + 1) * HALF)
+                nc.tensor.matmul(out=gp[:, cols], lhsT=ones[:], rhs=grow[:, cols], start=True, stop=True)
+            live["gp"] = gp
 
-        def gex(h, eng):
-            on(eng)(out=g_sb[:, h * HALF : (h + 1) * HALF], in_=live[("gp", h)][:])
+        def gex1(eng):
+            on(eng)(out=g_sb[:], in_=live["gp"][:])
+
+        def ggp():
+            nc.scalar.activation(out=junk_s[:, 0, :], in_=g8[:], func=ACT.Square, accum_out=gg_c[:])
+            nc.vector.tensor_scalar(out=gg_d[:], in0=ident[:, 0:H], scalar1=gg_c[:], scalar2=None, op0=ALU.mult)
+            gnp = psum.tile([P, H], F32, name="gnp", tag="bank")
+            nc.tensor.matmul(out=gnp[:], lhsT=ones_f[:], rhs=gg_d[:], start=True, stop=True)
+            nc.scalar.activation(out=gn_t[:, 0, :], in_=gnp[:], func=ACT.Sqrt, scale=float(H * H))
 
         def rg(s, c, h, eng):
             g = wg_pool.tile([P, 4 * HALF], BF16, name="wg", tag="wg", align_bytes=64)
-            src = wraw[s][:, c].rearrange("p u e n -> p (u e) n")[:, :, h * HALF : (h + 1) * HALF]
+            if s == 0:
+                src = wq_raw[:, c, h, :, :]
+            else:
+                src = (wk_raw if s == 1 else wv_raw)[:, c, :, h * HALF : (h + 1) * HALF]
             on(eng)(
                 out=g[:].rearrange("p (a i j) -> p a j i", i=4, j=4),
                 in_=src.rearrange("p j (a i) -> p a j i", i=4),
@@ -147,11 +168,10 @@ def tile_memeffattention_pa_kernel(tc, x, W_qkv, q_g, out_0, out_1, out_2, out_3
             on(eng)(out=xgw[:, t % 2], in_=live[("xt", t)][:].rearrange("p c u m -> p c m u"))
 
         def xq(t0, nt):
-            a = (t0 % 2) * 1024
             nc.vector.quantize_mx(
                 out=xc[:, t0 * 256 : (t0 + nt) * 256].bitcast(FP8X4),
                 scales=xs[:, t0 * 256 : (t0 + nt) * 256],
-                in_=live[("xg", t0 // 2)][:, a : a + nt * 1024],
+                in_=live[("xg", t0 // 2)][:, 0 : nt * 1024],
             )
 
         def mx(b):
@@ -186,38 +206,24 @@ def tile_memeffattention_pa_kernel(tc, x, W_qkv, q_g, out_0, out_1, out_2, out_3
             elif h == 1:
                 nc.sync.dma_start(out=outs[s][:, t, :], in_=row)
 
-        def dot_v(a, b, acc1, slot):
-            nc.vector.scalar_tensor_tensor(
-                out=junk_v[:, slot, :], in0=a, scalar=1.0, in1=b,
-                op0=ALU.mult, op1=ALU.mult, accum_out=acc1,
-            )
-
-        def gg(n):
-            for r in range(n):
-                hd = done["gg"]
-                done["gg"] = hd + 1
-                gh = g_sb[:, hd * D : (hd + 1) * D]
-                dot_v(gh, gh, gg_t[:, hd : hd + 1], hd)
-
         def dot(n):
-            for r in range(n):
-                k = done["dot"]
+            for k in range(done["dot"], min(done["dot"] + n, T * H)):
                 done["dot"] = k + 1
                 t, hd = k // H, k % H
-                dot_v(q_sb[:, t, hd * D : (hd + 1) * D], g_sb[:, hd * D : (hd + 1) * D], qd[:, k : k + 1], hd)
+                nc.vector.scalar_tensor_tensor(
+                    out=junk_v[:, hd, :], in0=q_sb[:, t, hd * D : (hd + 1) * D], scalar=1.0,
+                    in1=g_sb[:, hd * D : (hd + 1) * D], op0=ALU.mult, op1=ALU.mult,
+                    accum_out=qd[:, k : k + 1],
+                )
 
         def sq(n):
-            for r in range(n):
-                k = done["sq"]
+            for k in range(done["sq"], min(done["sq"] + n, T * H)):
                 done["sq"] = k + 1
                 t, hd = k // H, k % H
                 nc.scalar.activation(
                     out=junk_s[:, hd, :], in_=q_sb[:, t, hd * D : (hd + 1) * D], func=ACT.Square,
                     accum_out=qq[:, k : k + 1],
                 )
-
-        def gn():
-            nc.scalar.activation(out=gn_t[:, 0, :], in_=gg_t[:], func=ACT.Sqrt, scale=float(H * H))
 
         def qn():
             nc.scalar.activation(out=qn_t[:].rearrange("p t h -> p (t h)"), in_=qq[:], func=ACT.Sqrt)
@@ -251,226 +257,121 @@ def tile_memeffattention_pa_kernel(tc, x, W_qkv, q_g, out_0, out_1, out_2, out_3
                 in_=rows_t[1:8, :],
             )
 
-        ldw(0, 0, 0)
-        ldw(0, 0, 1)
-        ldw(0, 1, 0)
-        ldw(0, 1, 1)
-        ldx(0, 1)
-        ldx(1, 1)
-        ldx(2, 2)
-        ldx(4, 2)
-        ldx(6, 2)
-        ldw(1, 0, 0)
-        ldw(1, 0, 1)
-        ldw(1, 1, 0)
-        ldw(1, 1, 1)
+
+        for i in range(4):
+            ldwh(0, i % 2, i // 2)
+            ldx(2 * i, 2)
         ldg()
-        ldw(2, 0, 0)
-        ldw(2, 0, 1)
-        ldw(2, 1, 0)
-        ldw(2, 1, 1)
-        rg(0, 0, 0, "v")
-        rg(0, 0, 1, "s")
+        for s in (1, 2):
+            for c in (0, 1):
+                ldwc(s, c)
         masks()
-        qz(0, 0, 0)
-        rg(0, 1, 0, "v")
-        rg(0, 1, 1, "s")
-        qz(0, 0, 1)
-        qz(0, 1, 0)
+
+        rg(0, 0, 0, "v")
         xT(0)
         xT(1)
+        xe(0, "s")
+        xe(1, "s")
+        qz(0, 0, 0)
+        rg(0, 1, 0, "v")
+        xq(0, 2)
         xT(2)
         xT(3)
-        xT(4)
-        xT(5)
-        xe(0, "v")
-        xe(1, "s")
-        qz(0, 1, 1)
-        xq(0, 2)
-        mx(0)
-        mx(1)
         xe(2, "s")
         xe(3, "s")
+        qz(0, 1, 0)
+        mx(0)
         mx(2)
-        mx(3)
+        rg(0, 0, 1, "v")
         xq(2, 2)
-        xT(6)
-        xT(7)
+        xT(4)
+        xT(5)
+        mx(4)
+        mx(6)
+        ex(0, "s")
+        ex(2, "s")
         xe(4, "s")
         xe(5, "s")
+        xT(6)
+        xT(7)
+        rg(0, 1, 1, "v")
+        qz(0, 0, 1)
         xq(4, 2)
-        mx(4)
-        mx(5)
-        ex(0, "s")
-        mx(6)
-        ex(1, "s")
-        mx(7)
-        xe(6, "s")
-        xe(7, "v")
-        rg(1, 0, 0, "v")
-        ex(2, "s")
-        mx(8)
-        xq(6, 2)
-        ex(3, "s")
-        mx(9)
         ex(4, "s")
-        mx(10)
-        rg(1, 0, 1, "v")
-        ex(5, "s")
-        mx(11)
-        qz(1, 0, 0)
         ex(6, "s")
-        mx(12)
-        rg(1, 1, 0, "v")
-        gmm(0)
-        gmm(1)
-        ex(7, "s")
-        mx(13)
-        qz(1, 0, 1)
+        xe(6, "s")
+        xe(7, "s")
+        mx(8)
+        mx(10)
         ex(8, "s")
-        mx(14)
-        sq(2)
-        rg(1, 1, 1, "v")
-        gex(0, "s")
-        gex(1, "s")
-        ex(9, "s")
-        mx(15)
-        sq(2)
-        qz(1, 1, 0)
-        qz(1, 1, 1)
+        rg(1, 0, 0, "v")
+        qz(0, 1, 1)
+        mx(1)
+        mx(3)
+        mx(5)
+        mx(7)
         ex(10, "s")
-        mx(16)
-        sq(2)
-        ex(11, "s")
-        mx(17)
-        sq(2)
+        xq(6, 2)
+        ex(1, "s")
+        ex(3, "s")
+        rg(1, 1, 0, "v")
+        mx(12)
+        mx(14)
+        mx(9)
+        mx(11)
+        ex(5, "s")
+        ex(7, "s")
+        gmm1()
+        qz(1, 0, 0)
+        mx(13)
+        mx(15)
         ex(12, "s")
-        mx(18)
-        sq(2)
-        ex(13, "s")
-        mx(19)
-        sq(2)
         ex(14, "s")
-        mx(20)
-        sq(2)
-        ex(15, "s")
-        mx(21)
-        sq(2)
-        rg(2, 0, 0, "v")
-        gg(2)
-        rg(2, 1, 0, "v")
-        ex(16, "s")
-        mx(22)
-        sq(2)
-        qz(2, 0, 0)
-        gg(2)
-        ex(17, "s")
-        mx(23)
-        sq(2)
-        qz(2, 1, 0)
-        rg(2, 0, 1, "v")
-        ex(18, "s")
-        mx(24)
-        sq(2)
-        gg(2)
-        rg(2, 1, 1, "v")
-        ex(19, "s")
-        mx(25)
-        sq(2)
-        qz(2, 0, 1)
-        gg(2)
-        ex(20, "s")
-        mx(26)
-        sq(2)
-        qz(2, 1, 1)
-        ex(21, "s")
-        mx(27)
-        sq(2)
-        gn()
-        dot(3)
-        ex(22, "s")
-        mx(28)
-        sq(2)
-        dot(3)
-        ex(23, "v")
-        mx(29)
-        dot(3)
-        ex(24, "s")
-        mx(30)
-        sq(2)
-        dot(3)
-        ex(25, "s")
-        mx(31)
-        sq(2)
-        dot(3)
-        ex(26, "s")
-        mx(32)
-        sq(3)
-        dot(3)
-        ex(27, "v")
-        mx(33)
-        dot(3)
-        ex(28, "s")
-        mx(34)
-        sq(2)
-        dot(3)
-        ex(29, "s")
-        mx(35)
-        sq(3)
-        dot(3)
-        ex(30, "s")
-        mx(36)
-        sq(2)
-        dot(3)
-        ex(31, "v")
-        mx(37)
-        dot(3)
-        ex(32, "s")
-        mx(38)
-        sq(3)
-        dot(3)
-        ex(33, "s")
-        mx(39)
-        sq(2)
-        dot(3)
-        ex(34, "s")
-        mx(40)
-        sq(3)
-        dot(3)
-        ex(35, "v")
-        mx(41)
-        dot(3)
-        ex(36, "s")
-        mx(42)
-        sq(2)
-        dot(3)
-        ex(37, "s")
-        mx(43)
-        sq(3)
-        dot(3)
-        ex(38, "s")
-        mx(44)
-        sq(2)
-        dot(3)
-        ex(39, "v")
-        mx(45)
-        dot(3)
-        ex(40, "s")
-        mx(46)
-        sq(3)
-        dot(4)
-        ex(41, "s")
-        mx(47)
-        sq(2)
-        qn()
-        dot(3)
-        ex(42, "s")
-        ex(43, "v")
-        chain()
-        blk()
-        ex(44, "s")
-        rows("s")
-        stsim()
-        ex(45, "v")
-        ex(46, "s")
-        ex(47, "v")
+        ex(9, "s")
+        ex(11, "s")
+        gex1("s")
+        rg(1, 0, 1, "v")
+        qz(1, 1, 0)
+
+        prep = [
+            (rg, (1, 1, 1, "v")), (qz, (1, 0, 1)), (rg, (2, 0, 0, "v")), (qz, (1, 1, 1)), (rg, (2, 1, 0, "v")),
+            (qz, (2, 0, 0)), (rg, (2, 0, 1, "v")), (qz, (2, 1, 0)), (rg, (2, 1, 1, "v")), (qz, (2, 0, 1)),
+            (qz, (2, 1, 1)),
+        ]
+        k_banks = [16 + 2 * t for t in range(T)] + [17 + 2 * t for t in range(T)]
+        v_banks = list(range(32, 48))
+        ahead = k_banks + v_banks
+        before = {17: 4, 32: 11}
+        steps = 0
+        for i, b in enumerate([13, 15] + k_banks):
+            while steps < before.get(ahead[i], 0):
+                prep[steps][0](*prep[steps][1])
+                steps += 1
+            mx(ahead[i])
+            ex(b, "s")
+            if b == 20:
+                ggp()
+            if steps < len(prep):
+                prep[steps][0](*prep[steps][1])
+                steps += 1
+
+        for i, b in enumerate(v_banks):
+            if 18 + i < len(ahead):
+                mx(ahead[18 + i])
+            if i in (1, 4, 7, 10):
+                ex(b, "v")
+                dot(2)
+            else:
+                ex(b, "s")
+                dot(7)
+            sq(6)
+            if i == 10:
+                sq(64)
+                dot(64)
+                qn()
+            if i == 10:
+                chain()
+            if i == 14:
+                blk()
+                rows("s")
+                stsim()

@@ -31,7 +31,8 @@ def tile_memeffattention_pa_kernel(tc, x, W_qkv, q_g, out_0, out_1, out_2, out_3
         wg_pool = ctx.enter_context(tc.tile_pool(name="wg", bufs=4))
         xg_pool = ctx.enter_context(tc.tile_pool(name="xg", bufs=2))
         kv_pool = ctx.enter_context(tc.tile_pool(name="kv", bufs=12))
-        psum = ctx.enter_context(tc.psum_pool(name="psum", bufs=8))
+        psum_g = ctx.enter_context(tc.psum_pool(name="psum_g", bufs=1))
+        psum = ctx.enter_context(tc.psum_pool(name="psum", bufs=7))
         ctx.enter_context(tc.manual_schedule())
 
         xv = x.flatten_outer_dims().rearrange("(p t) k -> p t k", t=T)
@@ -70,7 +71,6 @@ def tile_memeffattention_pa_kernel(tc, x, W_qkv, q_g, out_0, out_1, out_2, out_3
         wc = const.tile([P, 3 * 2 * C], U32, name="wc", align_bytes=64)
         ws = const.tile([P, 3 * 2 * C], U8, name="ws", align_bytes=64)
         q_sb = const.tile([P, T, C], F32, name="q_sb")
-        g_sb = const.tile([P, C], BF16, name="g_sb")
         qq = const.tile([P, T * H], F32, name="qq")
         qd = const.tile([P, T * H], F32, name="qd")
         gg_c = const.tile([P, 1], F32, name="gg_c")
@@ -112,14 +112,11 @@ def tile_memeffattention_pa_kernel(tc, x, W_qkv, q_g, out_0, out_1, out_2, out_3
             )
 
         def gmm1():
-            gp = psum.tile([P, C], BF16, name="gp", tag="bank")
+            gp = psum_g.tile([P, C], BF16, name="gp", tag="gp")
             for h in range(2):
                 cols = slice(h * HALF, (h + 1) * HALF)
                 nc.tensor.matmul(out=gp[:, cols], lhsT=ones[:], rhs=grow[:, cols], start=True, stop=True)
             live["gp"] = gp
-
-        def gex1(eng):
-            on(eng)(out=g_sb[:], in_=live["gp"][:])
 
         def ggp():
             nc.scalar.activation(out=junk_s[:, 0, :], in_=g8[:], func=ACT.Square, accum_out=gg_c[:])
@@ -212,7 +209,7 @@ def tile_memeffattention_pa_kernel(tc, x, W_qkv, q_g, out_0, out_1, out_2, out_3
                 t, hd = k // H, k % H
                 nc.vector.scalar_tensor_tensor(
                     out=junk_v[:, hd, :], in0=q_sb[:, t, hd * D : (hd + 1) * D], scalar=1.0,
-                    in1=g_sb[:, hd * D : (hd + 1) * D], op0=ALU.mult, op1=ALU.mult,
+                    in1=live["gp"][:, hd * D : (hd + 1) * D], op0=ALU.mult, op1=ALU.mult,
                     accum_out=qd[:, k : k + 1],
                 )
 
@@ -329,7 +326,6 @@ def tile_memeffattention_pa_kernel(tc, x, W_qkv, q_g, out_0, out_1, out_2, out_3
         ex(14, "s")
         ex(9, "s")
         ex(11, "s")
-        gex1("s")
         rg(1, 0, 1, "v")
         qz(1, 1, 0)
 

@@ -62,7 +62,7 @@ def tile_memeffattention_pa_kernel(tc, x, W_qkv, q_g, out_0, out_1, out_2, out_3
         nc.vector.memset(ones_f[:], 1.0)
         warm = const.tile([P, 2], F32, name="warm")
         nc.vector.memset(warm[:], 1.0)
-        nc.scalar.activation(out=warm[:, 1:2], in_=warm[:, 0:1], func=ACT.Sqrt)
+        nc.scalar.activation(out=warm[:, 1:2], in_=warm[:, 0:1], func=ACT.Abs_reciprocal_sqrt)
         blk_m = const.tile([P, P], F32, name="blk_m")
         nc.vector.memset(blk_m[:], 0.0)
         lane = const.tile([P, 16, 1], F32, name="lane")
@@ -92,6 +92,10 @@ def tile_memeffattention_pa_kernel(tc, x, W_qkv, q_g, out_0, out_1, out_2, out_3
         def ldwh(s, c, h):
             nc.sync.dma_start(out=wq_raw[:, c, h, :, :], in_=w_rows(s, c)[:, :, h * HALF : (h + 1) * HALF])
 
+        def ldwq(s, c, h, lo, hi):
+            cols = slice(h * HALF + lo * P, h * HALF + hi * P)
+            nc.sync.dma_start(out=wq_raw[:, c, h, :, lo * P : hi * P], in_=w_rows(s, c)[:, :, cols])
+
         def ldwc(s, c):
             raw = wk_raw if s == 1 else wv_raw
             nc.sync.dma_start(out=raw[:, c, :, :], in_=w_rows(s, c))
@@ -118,24 +122,32 @@ def tile_memeffattention_pa_kernel(tc, x, W_qkv, q_g, out_0, out_1, out_2, out_3
                 nc.tensor.matmul(out=gp[:, cols], lhsT=ones[:], rhs=grow[:, cols], start=True, stop=True)
             live["gp"] = gp
 
-        def ggp():
+        def ggc():
             nc.scalar.activation(out=junk_s[:, 0, :], in_=g8[:], func=ACT.Square, accum_out=gg_c[:])
+
+        def ggd():
             nc.vector.tensor_scalar(out=gg_d[:], in0=ident[:, 0:H], scalar1=gg_c[:], scalar2=None, op0=ALU.mult)
+
+        def ggm():
             gnp = psum.tile([P, H], F32, name="gnp", tag="bank")
             nc.tensor.matmul(out=gnp[:], lhsT=ones_f[:], rhs=gg_d[:], start=True, stop=True)
-            nc.scalar.activation(out=gn_t[:, 0, :], in_=gnp[:], func=ACT.Sqrt, scale=float(H * H))
+            live["gnp"] = gnp
 
-        def rg(s, c, h, eng):
-            g = wg_pool.tile([P, 4 * HALF], BF16, name="wg", tag="wg", align_bytes=64)
+        def gnr():
+            nc.scalar.activation(out=gn_t[:, 0, :], in_=live["gnp"][:], func=ACT.Abs_reciprocal_sqrt, scale=float(H * H))
+
+        def rg(s, c, h, eng, lo=0, hi=4):
+            if ("wg", s, c, h) not in live:
+                live[("wg", s, c, h)] = wg_pool.tile([P, 4 * HALF], BF16, name="wg", tag="wg", align_bytes=64)
+            g = live[("wg", s, c, h)]
             if s == 0:
-                src = wq_raw[:, c, h, :, :]
+                src = wq_raw[:, c, h, :, lo * P : hi * P]
             else:
-                src = (wk_raw if s == 1 else wv_raw)[:, c, :, h * HALF : (h + 1) * HALF]
+                src = (wk_raw if s == 1 else wv_raw)[:, c, :, h * HALF + lo * P : h * HALF + hi * P]
             on(eng)(
-                out=g[:].rearrange("p (a i j) -> p a j i", i=4, j=4),
+                out=g[:, 4 * lo * P : 4 * hi * P].rearrange("p (a i j) -> p a j i", i=4, j=4),
                 in_=src.rearrange("p j (a i) -> p a j i", i=4),
             )
-            live[("wg", s, c, h)] = g
 
         def qz(s, c, h):
             o = (s * 2 + c) * C + h * HALF
@@ -223,14 +235,18 @@ def tile_memeffattention_pa_kernel(tc, x, W_qkv, q_g, out_0, out_1, out_2, out_3
                 )
 
         def qn():
-            nc.scalar.activation(out=qn_t[:].rearrange("p t h -> p (t h)"), in_=qq[:], func=ACT.Sqrt)
+            nc.scalar.activation(
+                out=qn_t[:].rearrange("p t h -> p (t h)"), in_=qq[:], func=ACT.Abs_reciprocal_sqrt
+            )
+
+        def qg():
+            nc.vector.tensor_tensor(
+                out=den[:], in0=qd[:].rearrange("p (t h) -> p t h", h=H),
+                in1=gn_t[:].to_broadcast([P, T, H]), op=ALU.mult,
+            )
 
         def chain():
-            nc.vector.tensor_tensor(out=den[:], in0=qn_t[:], in1=gn_t[:].to_broadcast([P, T, H]), op=ALU.mult)
-            nc.vector.reciprocal(out=den[:], in_=den[:])
-            nc.vector.tensor_tensor(
-                out=den[:], in0=den[:], in1=qd[:].rearrange("p (t h) -> p t h", h=H), op=ALU.mult
-            )
+            nc.vector.tensor_tensor(out=den[:], in0=den[:], in1=qn_t[:], op=ALU.mult)
             nc.vector.tensor_reduce(out=sim[:, 0, :], in_=den[:], axis=AX.X, op=ALU.add)
             nc.vector.tensor_tensor(
                 out=spread[:], in0=sim[:].to_broadcast([P, 16, T]), in1=lane[:].to_broadcast([P, 16, T]),
@@ -255,22 +271,30 @@ def tile_memeffattention_pa_kernel(tc, x, W_qkv, q_g, out_0, out_1, out_2, out_3
             )
 
 
-        for i in range(4):
-            ldwh(0, i % 2, i // 2)
-            ldx(2 * i, 2)
+        ldwq(0, 0, 0, 0, 2)
+        ldwq(0, 0, 0, 2, 4)
+        ldx(0, 2)
+        ldwh(0, 1, 0)
+        ldx(2, 2)
+        ldwh(0, 0, 1)
+        ldx(4, 2)
+        ldwh(0, 1, 1)
+        ldx(6, 2)
         ldg()
         for s in (1, 2):
             for c in (0, 1):
                 ldwc(s, c)
         masks()
 
-        rg(0, 0, 0, "v")
+        rg(0, 0, 0, "v", 0, 2)
+        rg(0, 0, 0, "s", 2, 4)
         xT(0)
         xT(1)
+        qz(0, 0, 0)
         xe(0, "s")
         xe(1, "s")
-        qz(0, 0, 0)
-        rg(0, 1, 0, "v")
+        rg(0, 1, 0, "v", 0, 3)
+        rg(0, 1, 0, "s", 3, 4)
         xq(0, 2)
         xT(2)
         xT(3)
@@ -298,20 +322,20 @@ def tile_memeffattention_pa_kernel(tc, x, W_qkv, q_g, out_0, out_1, out_2, out_3
         ex(6, "s")
         xe(6, "s")
         xe(7, "s")
+        qz(0, 1, 1)
         mx(8)
         mx(10)
-        ex(8, "s")
-        rg(1, 0, 0, "v")
-        qz(0, 1, 1)
         mx(1)
         mx(3)
-        mx(5)
-        mx(7)
+        ex(8, "s")
         ex(10, "s")
+        rg(1, 0, 0, "v")
         xq(6, 2)
         ex(1, "s")
         ex(3, "s")
         rg(1, 1, 0, "v")
+        mx(5)
+        mx(7)
         mx(12)
         mx(14)
         mx(9)
@@ -326,6 +350,7 @@ def tile_memeffattention_pa_kernel(tc, x, W_qkv, q_g, out_0, out_1, out_2, out_3
         ex(14, "s")
         ex(9, "s")
         ex(11, "s")
+        ggc()
         rg(1, 0, 1, "v")
         qz(1, 1, 0)
 
@@ -345,11 +370,11 @@ def tile_memeffattention_pa_kernel(tc, x, W_qkv, q_g, out_0, out_1, out_2, out_3
                 steps += 1
             mx(ahead[i])
             ex(b, "s")
-            if b == 20:
-                ggp()
             if steps < len(prep):
                 prep[steps][0](*prep[steps][1])
                 steps += 1
+        ggd()
+        ggm()
 
         for i, b in enumerate(v_banks):
             if 18 + i < len(ahead):
@@ -361,11 +386,13 @@ def tile_memeffattention_pa_kernel(tc, x, W_qkv, q_g, out_0, out_1, out_2, out_3
                 ex(b, "s")
                 dot(7)
             sq(6)
+            if i == 1:
+                gnr()
             if i == 10:
                 sq(64)
                 dot(64)
+                qg()
                 qn()
-            if i == 10:
                 chain()
             if i == 14:
                 blk()

@@ -21,6 +21,7 @@ REG = 5
 T = N_TOK // P
 HALF = 512
 FINE = 6
+NG = 4
 FLOPS = 2 * N_TOK * C * 3 * C
 
 
@@ -30,6 +31,7 @@ def tile_memeffattention_pa_kernel(tc, x, W_qkv, q_g, out_0, out_1, out_2, out_3
         const = ctx.enter_context(tc.tile_pool(name="const", bufs=1))
         wg_pool = ctx.enter_context(tc.tile_pool(name="wg", bufs=4))
         xg_pool = ctx.enter_context(tc.tile_pool(name="xg", bufs=2))
+        z_pool = ctx.enter_context(tc.tile_pool(name="z", bufs=2))
         kv_pool = ctx.enter_context(tc.tile_pool(name="kv", bufs=12))
         psum_g = ctx.enter_context(tc.psum_pool(name="psum_g", bufs=1))
         psum = ctx.enter_context(tc.psum_pool(name="psum", bufs=7))
@@ -71,6 +73,7 @@ def tile_memeffattention_pa_kernel(tc, x, W_qkv, q_g, out_0, out_1, out_2, out_3
         wc = const.tile([P, 3 * 2 * C], U32, name="wc", align_bytes=64)
         ws = const.tile([P, 3 * 2 * C], U8, name="ws", align_bytes=64)
         q_sb = const.tile([P, T, C], F32, name="q_sb")
+        g_sb = const.tile([P, C], BF16, name="g_sb")
         qq = const.tile([P, T * H], F32, name="qq")
         qd = const.tile([P, T * H], F32, name="qd")
         gg_c = const.tile([P, 1], F32, name="gg_c")
@@ -84,7 +87,7 @@ def tile_memeffattention_pa_kernel(tc, x, W_qkv, q_g, out_0, out_1, out_2, out_3
         spread = const.tile([P, 16, T], F32, name="spread")
         rows_t = const.tile([P, P], F32, name="rows_t")
         live = {}
-        done = {"sq": 0, "dot": 0}
+        done = {"sq": 0, "dot": NG * H}
 
         def w_rows(s, c):
             return W_qkv[512 * c : 512 * c + 512, s * C : (s + 1) * C].rearrange("(q j) n -> q j n", j=4)
@@ -224,6 +227,22 @@ def tile_memeffattention_pa_kernel(tc, x, W_qkv, q_g, out_0, out_1, out_2, out_3
                     in1=live["gp"][:, hd * D : (hd + 1) * D], op0=ALU.mult, op1=ALU.mult,
                     accum_out=qd[:, k : k + 1],
                 )
+
+        def ldgb():
+            nc.sync.dma_start(out=g_sb[:], in_=q_g.rearrange("h d -> (h d)").partition_broadcast(P))
+
+        def gprod(t):
+            z = z_pool.tile([P, C], F32, name="z", tag="z")
+            for h in range(2):
+                cols = slice(h * HALF, (h + 1) * HALF)
+                nc.gpsimd.tensor_tensor(out=z[:, cols], in0=q_sb[:, t, cols], in1=g_sb[:, cols], op=ALU.mult)
+            live[("z", t)] = z
+
+        def zred(t):
+            nc.vector.tensor_reduce(
+                out=qd[:, t * H : (t + 1) * H], in_=live[("z", t)][:].rearrange("p (h d) -> p h d", h=H),
+                axis=AX.X, op=ALU.add,
+            )
 
         def sq(n):
             for k in range(done["sq"], min(done["sq"] + n, T * H)):
@@ -370,21 +389,31 @@ def tile_memeffattention_pa_kernel(tc, x, W_qkv, q_g, out_0, out_1, out_2, out_3
                 steps += 1
             mx(ahead[i])
             ex(b, "s")
+            if b == 17:
+                ldgb()
             if steps < len(prep):
                 prep[steps][0](*prep[steps][1])
                 steps += 1
         ggd()
         ggm()
 
+        gprod(0)
+        gprod(1)
+        z_at = (3, 5, 8, 10)
         for i, b in enumerate(v_banks):
             if 18 + i < len(ahead):
                 mx(ahead[18 + i])
-            if i in (1, 4, 7, 10):
+            if i in (1, 3, 5, 7, 9, 10):
                 ex(b, "v")
                 dot(2)
             else:
                 ex(b, "s")
-                dot(7)
+                dot(5)
+            if i in z_at:
+                t = z_at.index(i)
+                zred(t)
+                if t + 2 < 4:
+                    gprod(t + 2)
             sq(6)
             if i == 1:
                 gnr()

@@ -31,7 +31,6 @@ def tile_memeffattention_pa_kernel(tc, x, W_qkv, q_g, out_0, out_1, out_2, out_3
         const = ctx.enter_context(tc.tile_pool(name="const", bufs=1))
         wg_pool = ctx.enter_context(tc.tile_pool(name="wg", bufs=4))
         xg_pool = ctx.enter_context(tc.tile_pool(name="xg", bufs=2))
-        z_pool = ctx.enter_context(tc.tile_pool(name="z", bufs=2))
         kv_pool = ctx.enter_context(tc.tile_pool(name="kv", bufs=12))
         psum_g = ctx.enter_context(tc.psum_pool(name="psum_g", bufs=1))
         psum = ctx.enter_context(tc.psum_pool(name="psum", bufs=7))
@@ -228,11 +227,11 @@ def tile_memeffattention_pa_kernel(tc, x, W_qkv, q_g, out_0, out_1, out_2, out_3
                     accum_out=qd[:, k : k + 1],
                 )
 
-        def ldgb():
-            nc.sync.dma_start(out=g_sb[:], in_=q_g.rearrange("h d -> (h d)").partition_broadcast(P))
+        def gcp():
+            nc.scalar.copy(out=g_sb[:], in_=live["gp"][:])
 
         def gprod(t):
-            z = z_pool.tile([P, C], F32, name="z", tag="z")
+            z = wg_pool.tile([P, C], F32, name="z", tag="wg", align_bytes=64)
             for h in range(2):
                 cols = slice(h * HALF, (h + 1) * HALF)
                 nc.gpsimd.tensor_tensor(out=z[:, cols], in0=q_sb[:, t, cols], in1=g_sb[:, cols], op=ALU.mult)
@@ -292,6 +291,7 @@ def tile_memeffattention_pa_kernel(tc, x, W_qkv, q_g, out_0, out_1, out_2, out_3
 
         ldwq(0, 0, 0, 0, 2)
         ldwq(0, 0, 0, 2, 4)
+        ldg()
         ldx(0, 2)
         ldwh(0, 1, 0)
         ldx(2, 2)
@@ -299,16 +299,16 @@ def tile_memeffattention_pa_kernel(tc, x, W_qkv, q_g, out_0, out_1, out_2, out_3
         ldx(4, 2)
         ldwh(0, 1, 1)
         ldx(6, 2)
-        ldg()
         for s in (1, 2):
             for c in (0, 1):
                 ldwc(s, c)
         masks()
-
+        gmm1()
         rg(0, 0, 0, "v", 0, 2)
         rg(0, 0, 0, "s", 2, 4)
         xT(0)
         xT(1)
+        gcp()
         qz(0, 0, 0)
         xe(0, "s")
         xe(1, "s")
@@ -361,7 +361,6 @@ def tile_memeffattention_pa_kernel(tc, x, W_qkv, q_g, out_0, out_1, out_2, out_3
         mx(11)
         ex(5, "s")
         ex(7, "s")
-        gmm1()
         qz(1, 0, 0)
         mx(13)
         mx(15)
@@ -389,17 +388,15 @@ def tile_memeffattention_pa_kernel(tc, x, W_qkv, q_g, out_0, out_1, out_2, out_3
                 steps += 1
             mx(ahead[i])
             ex(b, "s")
-            if b == 17:
-                ldgb()
             if steps < len(prep):
                 prep[steps][0](*prep[steps][1])
                 steps += 1
         ggd()
         ggm()
 
-        gprod(0)
-        gprod(1)
-        z_at = (3, 5, 8, 10)
+        for t in range(NG):
+            gprod(t)
+        z_at = (2, 4, 6, 8)
         for i, b in enumerate(v_banks):
             if 18 + i < len(ahead):
                 mx(ahead[18 + i])
@@ -410,10 +407,7 @@ def tile_memeffattention_pa_kernel(tc, x, W_qkv, q_g, out_0, out_1, out_2, out_3
                 ex(b, "s")
                 dot(5)
             if i in z_at:
-                t = z_at.index(i)
-                zred(t)
-                if t + 2 < 4:
-                    gprod(t + 2)
+                zred(z_at.index(i))
             sq(6)
             if i == 1:
                 gnr()

@@ -21,7 +21,7 @@ REG = 5
 T = N_TOK // P
 HALF = 512
 FINE = 6
-NG = 4
+NG = 5
 FLOPS = 2 * N_TOK * C * 3 * C
 
 
@@ -394,30 +394,33 @@ def tile_memeffattention_pa_kernel(tc, x, W_qkv, q_g, out_0, out_1, out_2, out_3
         ggd()
         ggm()
 
-        for t in range(NG):
+        for t in range(4):
             gprod(t)
-        z_at = (2, 4, 6, 8)
+        z_at = (2, 4, 6, 8, 10)
         for i, b in enumerate(v_banks):
             if 18 + i < len(ahead):
                 mx(ahead[18 + i])
-            if i in (1, 3, 5, 7, 9, 10):
+            if i in (1, 3, 5, 7, 8, 9, 11, 14):
                 ex(b, "v")
                 dot(2)
             else:
                 ex(b, "s")
-                dot(5)
+                dot(4)
             if i in z_at:
-                zred(z_at.index(i))
-            sq(6)
+                t = z_at.index(i)
+                zred(t)
+                if t + 4 < NG:
+                    gprod(t + 4)
+            sq(5)
             if i == 1:
                 gnr()
-            if i == 10:
+            if i == 11:
                 sq(64)
                 dot(64)
                 qg()
                 qn()
                 chain()
-            if i == 14:
+            if i == 15:
                 blk()
                 rows("s")
                 stsim()

@@ -20,7 +20,7 @@ D = 128
 REG = 5
 T = N_TOK // P
 HALF = 512
-FINE = 6
+FINE = 5
 NG = 5
 FLOPS = 2 * N_TOK * C * 3 * C
 
@@ -36,9 +36,9 @@ def tile_memeffattention_pa_kernel(tc, x, W_qkv, q_g, out_0, out_1, out_2, out_3
         psum = ctx.enter_context(tc.psum_pool(name="psum", bufs=7))
         ctx.enter_context(tc.manual_schedule())
 
-        xv = x.flatten_outer_dims().rearrange("(p t) k -> p t k", t=T)
+        xv = x.flatten_outer_dims().rearrange("(t p) k -> p t k", p=P)
         outs = [
-            o.rearrange("b n h d -> (b n) (h d)").rearrange("(p t) f -> p t f", t=T)
+            o.rearrange("b n h d -> (b n) (h d)").rearrange("(t p) f -> p t f", p=P)
             for o in (out_0, out_1, out_2)
         ]
 
@@ -64,9 +64,8 @@ def tile_memeffattention_pa_kernel(tc, x, W_qkv, q_g, out_0, out_1, out_2, out_3
         warm = const.tile([P, 2], F32, name="warm")
         nc.vector.memset(warm[:], 1.0)
         nc.scalar.activation(out=warm[:, 1:2], in_=warm[:, 0:1], func=ACT.Abs_reciprocal_sqrt)
-        blk_m = const.tile([P, P], F32, name="blk_m")
-        nc.vector.memset(blk_m[:], 0.0)
-        lane = const.tile([P, 16, 1], F32, name="lane")
+        sim = const.tile([P, P], F32, name="sim")
+        nc.vector.memset(sim[:], 0.0)
         xc = const.tile([P, T * 2 * P], U32, name="xc", align_bytes=64)
         xs = const.tile([P, T * 2 * P], U8, name="xs", align_bytes=64)
         wc = const.tile([P, 3 * 2 * C], U32, name="wc", align_bytes=64)
@@ -82,8 +81,6 @@ def tile_memeffattention_pa_kernel(tc, x, W_qkv, q_g, out_0, out_1, out_2, out_3
         gn_t = const.tile([P, 1, H], F32, name="gn_t")
         qn_t = const.tile([P, T, H], F32, name="qn_t")
         den = const.tile([P, T, H], F32, name="den")
-        sim = const.tile([P, 1, T], F32, name="sim")
-        spread = const.tile([P, 16, T], F32, name="spread")
         rows_t = const.tile([P, P], F32, name="rows_t")
         live = {}
         done = {"sq": 0, "dot": NG * H}
@@ -108,14 +105,6 @@ def tile_memeffattention_pa_kernel(tc, x, W_qkv, q_g, out_0, out_1, out_2, out_3
         def ldg():
             nc.sync.dma_start(out=grow[0:1, :], in_=q_g.rearrange("(o h) d -> o (h d)", o=1))
             nc.sync.dma_start(out=g8[0:H, :], in_=q_g)
-
-        def masks():
-            nc.vector.tensor_reduce(
-                out=blk_m[:, 0:8], in_=ident[:].rearrange("p (m b) -> p m b", b=16), axis=AX.X, op=ALU.add
-            )
-            nc.vector.tensor_reduce(
-                out=lane[:, :, 0], in_=ident[:].rearrange("p (m b) -> p b m", b=16), axis=AX.X, op=ALU.add
-            )
 
         def gmm1():
             gp = psum_g.tile([P, C], BF16, name="gp", tag="gp")
@@ -202,6 +191,30 @@ def tile_memeffattention_pa_kernel(tc, x, W_qkv, q_g, out_0, out_1, out_2, out_3
                 )
             live[("acc", b)] = acc
 
+        def mxh(b, r):
+            s, t, h = b // 16, (b % 16) // 2, b % 2
+            acc = psum.tile([P, HALF // 2], F32, name="acc", tag="bank")
+            for c in range(2):
+                xo = (t * 2 + c) * P
+                wo = (s * 2 + c) * C + h * HALF + r * (HALF // 2)
+                nc.tensor.matmul_mx(
+                    out=acc[:],
+                    lhsT=xc[:, xo : xo + P].bitcast(FP8X4),
+                    lhsT_scale=xs[:, xo : xo + P],
+                    rhs=wc[:, wo : wo + HALF // 2].bitcast(FP8X4),
+                    rhs_scale=ws[:, wo : wo + HALF // 2],
+                    start=(c == 0),
+                    stop=(c == 1),
+                )
+            live[("acch", b, r)] = acc
+
+        def exh(b, r, eng):
+            s, t, h = b // 16, (b % 16) // 2, b % 2
+            cols = slice(h * HALF + r * (HALF // 2), h * HALF + (r + 1) * (HALF // 2))
+            row = live[("st", s, t)][:]
+            on(eng)(out=row[:, cols], in_=live[("acch", b, r)][:])
+            nc.sync.dma_start(out=outs[s][:, t, cols], in_=row[:, cols])
+
         def ex(b, eng):
             s, t, h = b // 16, (b % 16) // 2, b % 2
             cols = slice(h * HALF, (h + 1) * HALF)
@@ -265,17 +278,11 @@ def tile_memeffattention_pa_kernel(tc, x, W_qkv, q_g, out_0, out_1, out_2, out_3
 
         def chain():
             nc.vector.tensor_tensor(out=den[:], in0=den[:], in1=qn_t[:], op=ALU.mult)
-            nc.vector.tensor_reduce(out=sim[:, 0, :], in_=den[:], axis=AX.X, op=ALU.add)
-            nc.vector.tensor_tensor(
-                out=spread[:], in0=sim[:].to_broadcast([P, 16, T]), in1=lane[:].to_broadcast([P, 16, T]),
-                op=ALU.mult,
-            )
+            nc.vector.tensor_reduce(out=sim[:, 0:T], in_=den[:], axis=AX.X, op=ALU.add)
 
-        def blk():
+        def turn():
             sp = psum.tile([P, P], F32, name="sp", tag="bank")
-            nc.tensor.matmul(
-                out=sp[:], lhsT=blk_m[:], rhs=spread[:].rearrange("p b t -> p (b t)"), start=True, stop=True
-            )
+            nc.tensor.transpose(sp[:], sim[:], ident[:])
             live["sp"] = sp
 
         def rows(eng):
@@ -302,7 +309,6 @@ def tile_memeffattention_pa_kernel(tc, x, W_qkv, q_g, out_0, out_1, out_2, out_3
         for s in (1, 2):
             for c in (0, 1):
                 ldwc(s, c)
-        masks()
         gmm1()
         rg(0, 0, 0, "v", 0, 2)
         rg(0, 0, 0, "s", 2, 4)
@@ -396,31 +402,35 @@ def tile_memeffattention_pa_kernel(tc, x, W_qkv, q_g, out_0, out_1, out_2, out_3
 
         for t in range(4):
             gprod(t)
-        z_at = (2, 4, 6, 8, 10)
-        for i, b in enumerate(v_banks):
-            if 18 + i < len(ahead):
+        z_at = (3, 5, 7, 9, 11)
+        for i, b in enumerate(v_banks[:-1]):
+            if 18 + i < len(ahead) - 1:
                 mx(ahead[18 + i])
-            if i in (1, 3, 5, 7, 8, 9, 11, 14):
+            if i == 13:
+                mxh(47, 0)
+                mxh(47, 1)
+            if i in (1, 3, 5, 7, 9, 11, 12, 14):
                 ex(b, "v")
                 dot(2)
             else:
                 ex(b, "s")
-                dot(4)
+                dot(2)
             if i in z_at:
                 t = z_at.index(i)
                 zred(t)
                 if t + 4 < NG:
                     gprod(t + 4)
-            sq(5)
+            sq(4)
             if i == 1:
                 gnr()
-            if i == 11:
+            if i == 12:
                 sq(64)
                 dot(64)
                 qg()
                 qn()
                 chain()
-            if i == 15:
-                blk()
-                rows("s")
-                stsim()
+        exh(47, 0, "s")
+        exh(47, 1, "v")
+        turn()
+        rows("s")
+        stsim()

from contextlib import ExitStack

import concourse.mybir as mybir
from concourse.masks import make_identity

F32 = mybir.dt.float32
BF16 = mybir.dt.bfloat16
U32 = mybir.dt.uint32
U8 = mybir.dt.uint8
FP8X4 = mybir.dt.float8_e4m3fn_x4
ACT = mybir.ActivationFunctionType
ALU = mybir.AluOpType
AX = mybir.AxisListType

P = 128
N_TOK = 1024
C = 1024
H = 8
D = 128
REG = 5
T = N_TOK // P
HALF = 512
FINE = 5
NG = 5
FLOPS = 2 * N_TOK * C * 3 * C


def tile_memeffattention_pa_kernel(tc, x, W_qkv, q_g, out_0, out_1, out_2, out_3):
    nc = tc.nc
    with ExitStack() as ctx:
        const = ctx.enter_context(tc.tile_pool(name="const", bufs=1))
        wg_pool = ctx.enter_context(tc.tile_pool(name="wg", bufs=4))
        xg_pool = ctx.enter_context(tc.tile_pool(name="xg", bufs=2))
        kv_pool = ctx.enter_context(tc.tile_pool(name="kv", bufs=12))
        psum_g = ctx.enter_context(tc.psum_pool(name="psum_g", bufs=1))
        psum = ctx.enter_context(tc.psum_pool(name="psum", bufs=7))
        ctx.enter_context(tc.manual_schedule())

        xv = x.flatten_outer_dims().rearrange("(t p) k -> p t k", p=P)
        outs = [
            o.rearrange("b n h d -> (b n) (h d)").rearrange("(t p) f -> p t f", p=P)
            for o in (out_0, out_1, out_2)
        ]

        def on(eng):
            return nc.vector.tensor_copy if eng == "v" else nc.scalar.copy

        grow = const.tile([P, C], BF16, name="grow")
        nc.vector.memset(grow[:], 0.0)
        g8 = const.tile([P, D], BF16, name="g8")
        nc.vector.memset(g8[:], 0.0)
        x_sb = const.tile([P, T * C], BF16, name="x_sb")
        x_sb3 = x_sb[:].rearrange("p (t k) -> p t k", t=T)
        xw = x_sb[:].bitcast(F32).rearrange("p (t w) -> p t w", t=T)
        wq_raw = const.tile([P, 2, 2, 4, HALF], BF16, name="wq_raw")
        wk_raw = const.tile([P, 2, 4, C], BF16, name="wk_raw")
        wv_raw = const.tile([P, 2, 4, C], BF16, name="wv_raw")
        ident = const.tile([P, P], F32, name="ident")
        make_identity(nc, ident[:])
        ones = const.tile([P, P], BF16, name="ones")
        nc.vector.memset(ones[:], 1.0)
        ones_f = const.tile([P, P], F32, name="ones_f")
        nc.vector.memset(ones_f[:], 1.0)
        warm = const.tile([P, 2], F32, name="warm")
        nc.vector.memset(warm[:], 1.0)
        nc.scalar.activation(out=warm[:, 1:2], in_=warm[:, 0:1], func=ACT.Abs_reciprocal_sqrt)
        sim = const.tile([P, P], F32, name="sim")
        nc.vector.memset(sim[:], 0.0)
        xc = const.tile([P, T * 2 * P], U32, name="xc", align_bytes=64)
        xs = const.tile([P, T * 2 * P], U8, name="xs", align_bytes=64)
        wc = const.tile([P, 3 * 2 * C], U32, name="wc", align_bytes=64)
        ws = const.tile([P, 3 * 2 * C], U8, name="ws", align_bytes=64)
        q_sb = const.tile([P, T, C], F32, name="q_sb")
        g_sb = const.tile([P, C], BF16, name="g_sb")
        qq = const.tile([P, T * H], F32, name="qq")
        qd = const.tile([P, T * H], F32, name="qd")
        gg_c = const.tile([P, 1], F32, name="gg_c")
        gg_d = const.tile([P, H], F32, name="gg_d")
        junk_s = const.tile([P, H, D], F32, name="junk_s")
        junk_v = const.tile([P, H, D], F32, name="junk_v")
        gn_t = const.tile([P, 1, H], F32, name="gn_t")
        qn_t = const.tile([P, T, H], F32, name="qn_t")
        den = const.tile([P, T, H], F32, name="den")
        rows_t = const.tile([P, P], F32, name="rows_t")
        live = {}
        done = {"sq": 0, "dot": NG * H}

        def w_rows(s, c):
            return W_qkv[512 * c : 512 * c + 512, s * C : (s + 1) * C].rearrange("(q j) n -> q j n", j=4)

        def ldwh(s, c, h):
            nc.sync.dma_start(out=wq_raw[:, c, h, :, :], in_=w_rows(s, c)[:, :, h * HALF : (h + 1) * HALF])

        def ldwq(s, c, h, lo, hi):
            cols = slice(h * HALF + lo * P, h * HALF + hi * P)
            nc.sync.dma_start(out=wq_raw[:, c, h, :, lo * P : hi * P], in_=w_rows(s, c)[:, :, cols])

        def ldwc(s, c):
            raw = wk_raw if s == 1 else wv_raw
            nc.sync.dma_start(out=raw[:, c, :, :], in_=w_rows(s, c))

        def ldx(t0, nt):
            nc.sync.dma_start(out=x_sb3[:, t0 : t0 + nt, :], in_=xv[:, t0 : t0 + nt, :])

        def ldg():
            nc.sync.dma_start(out=grow[0:1, :], in_=q_g.rearrange("(o h) d -> o (h d)", o=1))
            nc.sync.dma_start(out=g8[0:H, :], in_=q_g)

        def gmm1():
            gp = psum_g.tile([P, C], BF16, name="gp", tag="gp")
            for h in range(2):
                cols = slice(h * HALF, (h + 1) * HALF)
                nc.tensor.matmul(out=gp[:, cols], lhsT=ones[:], rhs=grow[:, cols], start=True, stop=True)
            live["gp"] = gp

        def ggc():
            nc.scalar.activation(out=junk_s[:, 0, :], in_=g8[:], func=ACT.Square, accum_out=gg_c[:])

        def ggd():
            nc.vector.tensor_scalar(out=gg_d[:], in0=ident[:, 0:H], scalar1=gg_c[:], scalar2=None, op0=ALU.mult)

        def ggm():
            gnp = psum.tile([P, H], F32, name="gnp", tag="bank")
            nc.tensor.matmul(out=gnp[:], lhsT=ones_f[:], rhs=gg_d[:], start=True, stop=True)
            live["gnp"] = gnp

        def gnr():
            nc.scalar.activation(out=gn_t[:, 0, :], in_=live["gnp"][:], func=ACT.Abs_reciprocal_sqrt, scale=float(H * H))

        def rg(s, c, h, eng, lo=0, hi=4):
            if ("wg", s, c, h) not in live:
                live[("wg", s, c, h)] = wg_pool.tile([P, 4 * HALF], BF16, name="wg", tag="wg", align_bytes=64)
            g = live[("wg", s, c, h)]
            if s == 0:
                src = wq_raw[:, c, h, :, lo * P : hi * P]
            else:
                src = (wk_raw if s == 1 else wv_raw)[:, c, :, h * HALF + lo * P : h * HALF + hi * P]
            on(eng)(
                out=g[:, 4 * lo * P : 4 * hi * P].rearrange("p (a i j) -> p a j i", i=4, j=4),
                in_=src.rearrange("p j (a i) -> p a j i", i=4),
            )

        def qz(s, c, h):
            o = (s * 2 + c) * C + h * HALF
            nc.vector.quantize_mx(
                out=wc[:, o : o + HALF].bitcast(FP8X4),
                scales=ws[:, o : o + HALF],
                in_=live[("wg", s, c, h)][:],
            )

        def xT(t):
            xt = psum.tile([P, 2, 2, P], F32, name="xt", tag="bank")
            for c in range(2):
                for u in range(2):
                    nc.tensor.transpose(
                        xt[:, c, u, :], xw[:, t, 256 * c + u : 256 * (c + 1) : 2], ident[:]
                    )
            live[("xt", t)] = xt

        def xe(t, eng):
            if t % 2 == 0:
                live[("xg", t // 2)] = xg_pool.tile(
                    [P, 2 * 2 * P * 4], BF16, name="xg", tag="xg", align_bytes=64
                )
            xgw = live[("xg", t // 2)][:].bitcast(F32).rearrange(
                "p (t c m u) -> p t c m u", t=2, c=2, u=2
            )
            on(eng)(out=xgw[:, t % 2], in_=live[("xt", t)][:].rearrange("p c u m -> p c m u"))

        def xq(t0, nt):
            nc.vector.quantize_mx(
                out=xc[:, t0 * 256 : (t0 + nt) * 256].bitcast(FP8X4),
                scales=xs[:, t0 * 256 : (t0 + nt) * 256],
                in_=live[("xg", t0 // 2)][:, 0 : nt * 1024],
            )

        def mx(b):
            s, t, h = b // 16, (b % 16) // 2, b % 2
            acc = psum.tile([P, HALF], F32, name="acc", tag="bank")
            for c in range(2):
                xo = (t * 2 + c) * P
                wo = (s * 2 + c) * C + h * HALF
                nc.tensor.matmul_mx(
                    out=acc[:],
                    lhsT=xc[:, xo : xo + P].bitcast(FP8X4),
                    lhsT_scale=xs[:, xo : xo + P],
                    rhs=wc[:, wo : wo + HALF].bitcast(FP8X4),
                    rhs_scale=ws[:, wo : wo + HALF],
                    start=(c == 0),
                    stop=(c == 1),
                )
            live[("acc", b)] = acc

        def mxh(b, r):
            s, t, h = b // 16, (b % 16) // 2, b % 2
            acc = psum.tile([P, HALF // 2], F32, name="acc", tag="bank")
            for c in range(2):
                xo = (t * 2 + c) * P
                wo = (s * 2 + c) * C + h * HALF + r * (HALF // 2)
                nc.tensor.matmul_mx(
                    out=acc[:],
                    lhsT=xc[:, xo : xo + P].bitcast(FP8X4),
                    lhsT_scale=xs[:, xo : xo + P],
                    rhs=wc[:, wo : wo + HALF // 2].bitcast(FP8X4),
                    rhs_scale=ws[:, wo : wo + HALF // 2],
                    start=(c == 0),
                    stop=(c == 1),
                )
            live[("acch", b, r)] = acc

        def exh(b, r, eng):
            s, t, h = b // 16, (b % 16) // 2, b % 2
            cols = slice(h * HALF + r * (HALF // 2), h * HALF + (r + 1) * (HALF // 2))
            row = live[("st", s, t)][:]
            on(eng)(out=row[:, cols], in_=live[("acch", b, r)][:])
            nc.sync.dma_start(out=outs[s][:, t, cols], in_=row[:, cols])

        def ex(b, eng):
            s, t, h = b // 16, (b % 16) // 2, b % 2
            cols = slice(h * HALF, (h + 1) * HALF)
            if s == 0:
                row = q_sb[:, t, :]
            else:
                if h == 0:
                    live[("st", s, t)] = kv_pool.tile([P, C], F32, name="stage", tag="stage")
                row = live[("st", s, t)][:]
            on(eng)(out=row[:, cols], in_=live[("acc", b)][:])
            if s == 2 and t >= FINE:
                nc.sync.dma_start(out=outs[s][:, t, cols], in_=row[:, cols])
            elif h == 1:
                nc.sync.dma_start(out=outs[s][:, t, :], in_=row)

        def dot(n):
            for k in range(done["dot"], min(done["dot"] + n, T * H)):
                done["dot"] = k + 1
                t, hd = k // H, k % H
                nc.vector.scalar_tensor_tensor(
                    out=junk_v[:, hd, :], in0=q_sb[:, t, hd * D : (hd + 1) * D], scalar=1.0,
                    in1=live["gp"][:, hd * D : (hd + 1) * D], op0=ALU.mult, op1=ALU.mult,
                    accum_out=qd[:, k : k + 1],
                )

        def gcp():
            nc.scalar.copy(out=g_sb[:], in_=live["gp"][:])

        def gprod(t):
            z = wg_pool.tile([P, C], F32, name="z", tag="wg", align_bytes=64)
            for h in range(2):
                cols = slice(h * HALF, (h + 1) * HALF)
                nc.gpsimd.tensor_tensor(out=z[:, cols], in0=q_sb[:, t, cols], in1=g_sb[:, cols], op=ALU.mult)
            live[("z", t)] = z

        def zred(t):
            nc.vector.tensor_reduce(
                out=qd[:, t * H : (t + 1) * H], in_=live[("z", t)][:].rearrange("p (h d) -> p h d", h=H),
                axis=AX.X, op=ALU.add,
            )

        def sq(n):
            for k in range(done["sq"], min(done["sq"] + n, T * H)):
                done["sq"] = k + 1
                t, hd = k // H, k % H
                nc.scalar.activation(
                    out=junk_s[:, hd, :], in_=q_sb[:, t, hd * D : (hd + 1) * D], func=ACT.Square,
                    accum_out=qq[:, k : k + 1],
                )

        def qn():
            nc.scalar.activation(
                out=qn_t[:].rearrange("p t h -> p (t h)"), in_=qq[:], func=ACT.Abs_reciprocal_sqrt
            )

        def qg():
            nc.vector.tensor_tensor(
                out=den[:], in0=qd[:].rearrange("p (t h) -> p t h", h=H),
                in1=gn_t[:].to_broadcast([P, T, H]), op=ALU.mult,
            )

        def chain():
            nc.vector.tensor_tensor(out=den[:], in0=den[:], in1=qn_t[:], op=ALU.mult)
            nc.vector.tensor_reduce(out=sim[:, 0:T], in_=den[:], axis=AX.X, op=ALU.add)

        def turn():
            sp = psum.tile([P, P], F32, name="sp", tag="bank")
            nc.tensor.transpose(sp[:], sim[:], ident[:])
            live["sp"] = sp

        def rows(eng):
            on(eng)(out=rows_t[:], in_=live["sp"][:])

        def stsim():
            nc.sync.dma_start(out=out_3[0:1, 0 : P - REG], in_=rows_t[0:1, REG:P])
            nc.sync.dma_start(
                out=out_3[0:1, P - REG : N_TOK - REG].rearrange("o (m j) -> (o m) j", j=P),
                in_=rows_t[1:8, :],
            )


        ldwq(0, 0, 0, 0, 2)
        ldwq(0, 0, 0, 2, 4)
        ldg()
        ldx(0, 2)
        ldwh(0, 1, 0)
        ldx(2, 2)
        ldwh(0, 0, 1)
        ldx(4, 2)
        ldwh(0, 1, 1)
        ldx(6, 2)
        for s in (1, 2):
            for c in (0, 1):
                ldwc(s, c)
        gmm1()
        rg(0, 0, 0, "v", 0, 2)
        rg(0, 0, 0, "s", 2, 4)
        xT(0)
        xT(1)
        gcp()
        qz(0, 0, 0)
        xe(0, "s")
        xe(1, "s")
        rg(0, 1, 0, "v", 0, 3)
        rg(0, 1, 0, "s", 3, 4)
        xq(0, 2)
        xT(2)
        xT(3)
        xe(2, "s")
        xe(3, "s")
        qz(0, 1, 0)
        mx(0)
        mx(2)
        rg(0, 0, 1, "v")
        xq(2, 2)
        xT(4)
        xT(5)
        mx(4)
        mx(6)
        ex(0, "s")
        ex(2, "s")
        xe(4, "s")
        xe(5, "s")
        xT(6)
        xT(7)
        rg(0, 1, 1, "v")
        qz(0, 0, 1)
        xq(4, 2)
        ex(4, "s")
        ex(6, "s")
        xe(6, "s")
        xe(7, "s")
        qz(0, 1, 1)
        mx(8)
        mx(10)
        mx(1)
        mx(3)
        ex(8, "s")
        ex(10, "s")
        rg(1, 0, 0, "v")
        xq(6, 2)
        ex(1, "s")
        ex(3, "s")
        rg(1, 1, 0, "v")
        mx(5)
        mx(7)
        mx(12)
        mx(14)
        mx(9)
        mx(11)
        ex(5, "s")
        ex(7, "s")
        qz(1, 0, 0)
        mx(13)
        mx(15)
        ex(12, "s")
        ex(14, "s")
        ex(9, "s")
        ex(11, "s")
        ggc()
        rg(1, 0, 1, "v")
        qz(1, 1, 0)

        prep = [
            (rg, (1, 1, 1, "v")), (qz, (1, 0, 1)), (rg, (2, 0, 0, "v")), (qz, (1, 1, 1)), (rg, (2, 1, 0, "v")),
            (qz, (2, 0, 0)), (rg, (2, 0, 1, "v")), (qz, (2, 1, 0)), (rg, (2, 1, 1, "v")), (qz, (2, 0, 1)),
            (qz, (2, 1, 1)),
        ]
        k_banks = [16 + 2 * t for t in range(T)] + [17 + 2 * t for t in range(T)]
        v_banks = list(range(32, 48))
        ahead = k_banks + v_banks
        before = {17: 4, 32: 11}
        steps = 0
        for i, b in enumerate([13, 15] + k_banks):
            while steps < before.get(ahead[i], 0):
                prep[steps][0](*prep[steps][1])
                steps += 1
            mx(ahead[i])
            ex(b, "s")
            if steps < len(prep):
                prep[steps][0](*prep[steps][1])
                steps += 1
        ggd()
        ggm()

        for t in range(4):
            gprod(t)
        z_at = (3, 5, 7, 9, 11)
        for i, b in enumerate(v_banks[:-1]):
            if 18 + i < len(ahead) - 1:
                mx(ahead[18 + i])
            if i == 13:
                mxh(47, 0)
                mxh(47, 1)
            if i in (1, 3, 5, 7, 9, 11, 12, 14):
                ex(b, "v")
                dot(2)
            else:
                ex(b, "s")
                dot(2)
            if i in z_at:
                t = z_at.index(i)
                zred(t)
                if t + 4 < NG:
                    gprod(t + 4)
            sq(4)
            if i == 1:
                gnr()
            if i == 12:
                sq(64)
                dot(64)
                qg()
                qn()
                chain()
        exh(47, 0, "s")
        exh(47, 1, "v")
        turn()
        rows("s")
        stsim()
